import numpy as np
import ml_dtypes


def mxq(x, axis, fmt="e4m3"):
    dtype, down = {"e4m3": (ml_dtypes.float8_e4m3fn, 7), "e5m2": (ml_dtypes.float8_e5m2, 14)}[fmt]
    v = np.moveaxis(np.asarray(x, np.float32).astype(ml_dtypes.bfloat16).astype(np.float64), axis, -1)
    blocks = v.reshape(v.shape[:-1] + (-1, 32))
    amax = np.abs(blocks).max(-1, keepdims=True)
    byte = np.maximum(np.where(amax > 0, np.frexp(amax)[1] - 1 + 127, 0) - down, 1)
    scale = np.exp2(byte - 127.0)
    codes = (blocks / scale).astype(np.float32).astype(dtype).astype(np.float64)
    return np.moveaxis((codes * scale).reshape(v.shape), -1, axis)


WIDE = False


def mx_kscale(k):
    if not WIDE:
        return np.ones(k)
    levels = np.array([10, -10, 5, -5, 0])
    a = np.random.permutation(np.resize(levels, k // 512 * 4)).reshape(k // 512, 4)
    idx = np.arange(k)
    return np.exp2(a[idx // 512, idx % 128 // 32])


BF16 = ml_dtypes.bfloat16


def bf(x):
    return np.asarray(x, np.float32).astype(BF16)


def f64(x):
    return np.asarray(x).astype(np.float64)


E2M1 = np.array([0.0, 0.5, 1.0, 1.5, 2.0, 3.0, 4.0, 6.0, -0.0, -0.5, -1.0, -1.5, -2.0, -3.0, -4.0, -6.0])


def pack_weight(w, fmt):
    k, n = w.shape
    w = f64(bf(w)).reshape(k // 32, 32, n)
    amax = np.abs(w).max(1)
    if fmt == "e4m3":
        byte = np.frexp(amax)[1] - 1 + 127 - 7
    else:
        mant, ex = np.frexp(amax / 6.0)
        byte = np.where(mant > 0.5, ex, ex - 1) + 127
    byte = np.clip(np.where(amax > 0, byte, 1), 1, 254)
    scaled = (w * np.exp2(127.0 - byte)[:, None, :]).reshape(k, n).astype(np.float32)
    by_word = np.ascontiguousarray(scaled.reshape(k // 512, 128, 4, n).transpose(0, 1, 3, 2))
    if fmt == "e4m3":
        words = by_word.astype(ml_dtypes.float8_e4m3fn).view(np.uint8)
    else:
        c = by_word.astype(ml_dtypes.float4_e2m1fn).view(np.uint8) & 0xF
        words = c[..., 0::2] | (c[..., 1::2] << 4)
    return np.ascontiguousarray(words), np.ascontiguousarray(byte.astype(np.uint8).reshape(k // 512, 16, n))


def unpack_weight(words, scales, fmt):
    g, p, n, _ = words.shape
    if fmt == "e4m3":
        vals = np.ascontiguousarray(words).view(ml_dtypes.float8_e4m3fn).astype(np.float64)
    else:
        nib = np.empty((g, p, n, 4), np.uint8)
        nib[..., 0::2] = words & 0xF
        nib[..., 1::2] = words >> 4
        vals = E2M1[nib]
    vals = vals * np.repeat(np.exp2(scales.astype(np.float64) - 127.0), 8, axis=1)[..., None]
    return vals.transpose(0, 1, 3, 2).reshape(g * 512, n)


N, NR, F, C, R = 128, 2048, 8192, 128, 8
EPS = 1e-8
FMT = "e4m3"


def encode_amplitude(v):
    return v / (np.linalg.norm(v, axis=1, keepdims=True) + EPS)


def setup_inputs():
    s = mx_kscale(F)
    basis = np.random.standard_normal((R, F)) / np.sqrt(R)
    x = np.random.standard_normal((N, R)) @ basis + 0.5 * np.random.standard_normal((N, F))
    x_ref = np.random.standard_normal((NR, R)) @ basis + 0.5 * np.random.standard_normal((NR, F))
    c = 2.0 ** np.round(np.log2(np.mean(s ** 2) * np.mean(s ** -2.0)))
    mean_ = bf(np.random.standard_normal(F) * 0.5 * np.minimum(s, 1.0 / s))
    components_ = np.random.standard_normal((C, NR)) * 8.0 / np.sqrt(NR) * c
    words, scales = pack_weight(components_.T, FMT)
    return {"x": bf(x * s), "x_ref": bf(x_ref / s),
            "mean_": mean_,
            "components__words": words, "components__scales": scales}


def reference(x, x_ref, mean_, components__words, components__scales):
    xs = f64(x) - f64(mean_)
    xr = f64(x_ref) - f64(mean_)
    s1 = encode_amplitude(xs)
    s2 = encode_amplitude(xr)
    ov = mxq(s1, 1, "e4m3") @ mxq(s2, 1, "e4m3").T
    K = ov * ov
    return mxq(K, 1, "e4m3") @ unpack_weight(components__words, components__scales, FMT)

@@ -1,0 +1,245 @@
+from contextlib import ExitStack
+
+import concourse.mybir as mybir
+from concourse.masks import make_identity
+
+F32 = mybir.dt.float32
+BF16 = mybir.dt.bfloat16
+I32 = mybir.dt.int32
+U32 = mybir.dt.uint32
+U8 = mybir.dt.uint8
+FP8X4 = mybir.dt.float8_e4m3fn_x4
+ACT = mybir.ActivationFunctionType
+
+P = 128
+PACK = 4
+K_PASS = P * PACK
+
+X_ROWS = 128
+REF_ROWS = 2048
+FEATURES = 8192
+COMPONENTS = 128
+EPS = 1e-8
+
+FEATURE_PASSES = FEATURES // K_PASS
+REF_PASSES = REF_ROWS // K_PASS
+ROW_TILES = 1 + REF_ROWS // P
+
+CHUNK = 2048
+CHUNKS = FEATURES // CHUNK
+CHUNK_PASSES = CHUNK // K_PASS
+PAIR = 2
+BANK_PASSES = 2
+
+SCALAR_COLUMNS = PAIR * P
+VECTOR_COLUMNS = CHUNK - SCALAR_COLUMNS
+
+CENTRED_TILES = 3
+NORMALISE_LAG = (CENTRED_TILES - 1) * CHUNKS
+QUANTISE_LAG = NORMALISE_LAG + 1
+PROJECT_LAG = QUANTISE_LAG + 1
+
+FLOPS = 2 * X_ROWS * REF_ROWS * FEATURES + 2 * X_ROWS * REF_ROWS * COMPONENTS
+
+
+def tile_quantumkernelpca_w_kernel(
+    tc, x, x_ref, mean_, components__words, components__scales, out
+):
+    nc = tc.nc
+
+    ref_tiles = x_ref.rearrange("(g p t) f -> g t p f", p=P, t=PACK)
+    row_tiles = [x] + [ref_tiles[g, t] for g in range(REF_PASSES) for t in range(PACK)]
+
+    with ExitStack() as ctx:
+        const = ctx.enter_context(tc.tile_pool(name="const", bufs=1))
+        raw_pool = ctx.enter_context(tc.tile_pool(name="raw", bufs=8))
+        centred_pool = ctx.enter_context(tc.tile_pool(name="centred", bufs=CENTRED_TILES))
+        squares_pool = ctx.enter_context(tc.tile_pool(name="squares", bufs=2))
+        stat_pool = ctx.enter_context(tc.tile_pool(name="stat", bufs=3))
+        unit_pool = ctx.enter_context(tc.tile_pool(name="unit", bufs=3))
+        grouped_pool = ctx.enter_context(tc.tile_pool(name="grouped", bufs=3))
+        codes_pool = ctx.enter_context(tc.tile_pool(name="codes", bufs=2))
+        kernel_pool = ctx.enter_context(tc.tile_pool(name="kernel", bufs=2))
+        transpose_psum = ctx.enter_context(tc.psum_pool(name="transpose_psum", bufs=4))
+        overlap_psum = ctx.enter_context(tc.psum_pool(name="overlap_psum", bufs=2))
+        projection_psum = ctx.enter_context(tc.psum_pool(name="projection_psum", bufs=1))
+
+        identity = const.tile([P, P], F32)
+        make_identity(nc, identity[:])
+
+        mean_all = const.tile([P, FEATURES], BF16)
+        x_codes = const.tile([P, FEATURE_PASSES * X_ROWS], U32, align_bytes=64)
+        x_scales = const.tile([P, FEATURE_PASSES * X_ROWS], U8, align_bytes=64)
+        w_codes = const.tile([P, REF_PASSES * COMPONENTS], U32, align_bytes=64)
+        w_scales = const.tile([P, REF_PASSES * COMPONENTS], U8, align_bytes=64)
+        projection = projection_psum.tile([X_ROWS, COMPONENTS], F32)
+
+        nc.vector.memset(w_scales[:].bitcast(I32), 0)
+
+        work = {}
+
+        def load_weight():
+            nc.sync.dma_start(
+                out=w_codes[:].bitcast(I32).rearrange("p (g n) -> p g n", g=REF_PASSES),
+                in_=components__words.rearrange("g p n t -> p g (n t)").bitcast(I32),
+            )
+            for quadrant in range(4):
+                nc.sync.dma_start(
+                    out=w_scales[32 * quadrant : 32 * quadrant + 4, :]
+                    .bitcast(I32)
+                    .rearrange("q (g n) -> q g n", g=REF_PASSES),
+                    in_=components__scales[:, 4 * quadrant : 4 * quadrant + 4, :]
+                    .rearrange("g q n -> q g n")
+                    .bitcast(I32),
+                )
+
+        def centre_and_square(i, c):
+            cols = slice(c * CHUNK, (c + 1) * CHUNK)
+            if c == 0:
+                centred = centred_pool.tile([P, FEATURES], F32)
+                sums = stat_pool.tile([P, CHUNKS], F32)
+                work[i] = {"centred": centred, "sums": sums, "grouped": {}}
+            if i == 0:
+                nc.sync.dma_start(out=mean_all[:, cols], in_=mean_[cols].partition_broadcast(P))
+            raw = raw_pool.tile([P, CHUNK], BF16)
+            nc.sync.dma_start(out=raw[:], in_=row_tiles[i][:, cols])
+            nc.vector.tensor_sub(out=work[i]["centred"][:, cols], in0=raw[:], in1=mean_all[:, cols])
+            squares = squares_pool.tile([P, CHUNK], BF16)
+            nc.scalar.activation(
+                out=squares[:],
+                in_=work[i]["centred"][:, cols],
+                func=ACT.Square,
+                accum_out=work[i]["sums"][:, c : c + 1],
+            )
+
+        def row_norm(i):
+            sums_again = stat_pool.tile([P, CHUNKS], F32)
+            total = stat_pool.tile([P, 1], F32)
+            nc.scalar.activation(
+                out=sums_again[:], in_=work[i]["sums"][:], func=ACT.Copy, accum_out=total[:]
+            )
+            norm = stat_pool.tile([P, 1], F32)
+            nc.scalar.activation(out=norm[:], in_=total[:], func=ACT.Sqrt)
+            work[i]["norm"] = norm
+
+        def normalise_and_transpose(i, c):
+            if c == 0:
+                inverse = stat_pool.tile([P, 1], F32)
+                nc.vector.tensor_scalar_add(out=inverse[:], in0=work[i]["norm"][:], scalar1=EPS)
+                nc.vector.reciprocal(out=inverse[:], in_=inverse[:])
+                work[i]["inverse"] = inverse
+            unit = unit_pool.tile([P, CHUNK], BF16)
+            split = c * CHUNK + VECTOR_COLUMNS
+            nc.vector.tensor_scalar_mul(
+                out=unit[:, :VECTOR_COLUMNS],
+                in0=work[i]["centred"][:, c * CHUNK : split],
+                scalar1=work[i]["inverse"][:, 0:1],
+            )
+            nc.scalar.activation(
+                out=unit[:, VECTOR_COLUMNS:],
+                in_=work[i]["centred"][:, split : (c + 1) * CHUNK],
+                func=ACT.Copy,
+                scale=work[i]["inverse"][:, 0:1],
+            )
+            unit_words = unit[:].bitcast(F32)
+            grouped = grouped_pool.tile([P, CHUNK], BF16, align_bytes=64)
+            grouped_words = grouped[:].bitcast(F32).rearrange(
+                "p (g r u) -> p g r u", g=CHUNK_PASSES, u=PAIR
+            )
+            for first in range(0, CHUNK_PASSES, BANK_PASSES):
+                bank = transpose_psum.tile([P, BANK_PASSES, PAIR, P], F32)
+                for g in range(BANK_PASSES):
+                    for u in range(PAIR):
+                        start = ((first + g) * PAIR + u) * P
+                        nc.tensor.transpose(
+                            bank[:, g, u, :], unit_words[:, start : start + P], identity[:]
+                        )
+                nc.scalar.copy(
+                    out=grouped_words[:, first : first + BANK_PASSES],
+                    in_=bank[:].rearrange("p g u r -> p g r u"),
+                )
+            work[i]["grouped"][c] = grouped
+
+        def quantise_and_multiply(i, c):
+            if c == 0:
+                if i == 0:
+                    work[i]["codes"], work[i]["scales"] = x_codes, x_scales
+                else:
+                    codes = codes_pool.tile([P, FEATURE_PASSES * P], U32, align_bytes=64)
+                    scales = codes_pool.tile([P, FEATURE_PASSES * P], U8, align_bytes=64)
+                    overlap = overlap_psum.tile([P, X_ROWS], F32)
+                    work[i]["codes"], work[i]["scales"], work[i]["overlap"] = codes, scales, overlap
+            codes, scales = work[i]["codes"], work[i]["scales"]
+            chunk_words = slice(c * CHUNK_PASSES * P, (c + 1) * CHUNK_PASSES * P)
+            nc.vector.quantize_mx(
+                out=codes[:, chunk_words].bitcast(FP8X4),
+                scales=scales[:, chunk_words],
+                in_=work[i]["grouped"][c][:],
+            )
+            if i == 0:
+                return
+            for g in range(c * CHUNK_PASSES, (c + 1) * CHUNK_PASSES):
+                pass_words = slice(g * P, (g + 1) * P)
+                nc.tensor.matmul_mx(
+                    out=work[i]["overlap"][:],
+                    lhsT=codes[:, pass_words].bitcast(FP8X4),
+                    lhsT_scale=scales[:, pass_words],
+                    rhs=x_codes[:, pass_words].bitcast(FP8X4),
+                    rhs_scale=x_scales[:, pass_words],
+                    start=(g == 0),
+                    stop=(g == FEATURE_PASSES - 1),
+                )
+
+        def square_overlaps(i):
+            g, t = divmod(i - 1, PACK)
+            if t == 0:
+                kernel_grouped = kernel_pool.tile([P, X_ROWS, PACK], BF16, align_bytes=64)
+                work["kernel", g] = kernel_grouped
+            nc.scalar.activation(
+                out=work["kernel", g][:, :, t], in_=work[i]["overlap"][:], func=ACT.Square
+            )
+
+        def project(g):
+            kernel_codes = kernel_pool.tile([P, X_ROWS], U32, align_bytes=64)
+            kernel_scales = kernel_pool.tile([P, X_ROWS], U8, align_bytes=64)
+            nc.vector.quantize_mx(
+                out=kernel_codes[:].bitcast(FP8X4),
+                scales=kernel_scales[:],
+                in_=work["kernel", g][:].rearrange("p n t -> p (n t)"),
+            )
+            pass_words = slice(g * COMPONENTS, (g + 1) * COMPONENTS)
+            nc.tensor.matmul_mx(
+                out=projection[:],
+                lhsT=kernel_codes[:].bitcast(FP8X4),
+                lhsT_scale=kernel_scales[:],
+                rhs=w_codes[:, pass_words].bitcast(FP8X4),
+                rhs_scale=w_scales[:, pass_words],
+                start=(g == 0),
+                stop=(g == REF_PASSES - 1),
+            )
+
+        chunks = [(i, c) for i in range(ROW_TILES) for c in range(CHUNKS)]
+        for step in range(len(chunks) + PROJECT_LAG):
+            if step < len(chunks):
+                i, c = chunks[step]
+                centre_and_square(i, c)
+                if c == CHUNKS - 1:
+                    row_norm(i)
+                if step == CHUNKS:
+                    load_weight()
+            if 0 <= step - NORMALISE_LAG < len(chunks):
+                i, c = chunks[step - NORMALISE_LAG]
+                normalise_and_transpose(i, c)
+            if 0 <= step - QUANTISE_LAG < len(chunks):
+                i, c = chunks[step - QUANTISE_LAG]
+                quantise_and_multiply(i, c)
+                if i > 0 and c == CHUNKS - 1:
+                    square_overlaps(i)
+            if 0 <= step - PROJECT_LAG < len(chunks):
+                i, c = chunks[step - PROJECT_LAG]
+                if i > 0 and i % PACK == 0 and c == CHUNKS - 1:
+                    project(i // PACK - 1)
+
+        result = const.tile([X_ROWS, COMPONENTS], F32)
+        nc.vector.tensor_copy(out=result[:], in_=projection[:])
+        nc.sync.dma_start(out=out, in_=result[:])

@@ -10,6 +10,7 @@ U32 = mybir.dt.uint32
 U8 = mybir.dt.uint8
 FP8X4 = mybir.dt.float8_e4m3fn_x4
 ACT = mybir.ActivationFunctionType
+ALU = mybir.AluOpType
 
 P = 128
 PACK = 4
@@ -31,8 +32,14 @@ CHUNK_PASSES = CHUNK // K_PASS
 PAIR = 2
 BANK_PASSES = 2
 
-SCALAR_COLUMNS = PAIR * P
-VECTOR_COLUMNS = CHUNK - SCALAR_COLUMNS
+WORDS = FEATURES // PAIR
+WORD_BLOCKS = WORDS // P
+HALF = PAIR * 512
+HALVES = CHUNK // HALF
+HALF_BLOCKS = HALF // (PAIR * P)
+CHUNK_BLOCKS = CHUNK // (PAIR * P)
+MEAN_BANKS = 3
+SCALE_COLUMNS = 1024
 
 CENTRED_TILES = 3
 NORMALISE_LAG = (CENTRED_TILES - 1) * CHUNKS
@@ -60,19 +67,26 @@ def tile_quantumkernelpca_w_kernel(
         grouped_pool = ctx.enter_context(tc.tile_pool(name="grouped", bufs=3))
         codes_pool = ctx.enter_context(tc.tile_pool(name="codes", bufs=2))
         kernel_pool = ctx.enter_context(tc.tile_pool(name="kernel", bufs=2))
-        transpose_psum = ctx.enter_context(tc.psum_pool(name="transpose_psum", bufs=4))
+        transpose_psum = ctx.enter_context(tc.psum_pool(name="transpose_psum", bufs=3))
+        mean_psum = ctx.enter_context(tc.psum_pool(name="mean_psum", bufs=MEAN_BANKS))
         overlap_psum = ctx.enter_context(tc.psum_pool(name="overlap_psum", bufs=2))
-        projection_psum = ctx.enter_context(tc.psum_pool(name="projection_psum", bufs=1))
 
+        mean_rows = const.tile([P, PAIR * P], BF16)
+        nc.vector.memset(mean_rows[:], 0.0)
+        nc.sync.dma_start(
+            out=mean_rows[:WORD_BLOCKS, :], in_=mean_.rearrange("(b w) -> b w", b=WORD_BLOCKS)
+        )
         identity = const.tile([P, P], F32)
         make_identity(nc, identity[:])
 
-        mean_all = const.tile([P, FEATURES], BF16)
+        mean_words = const.tile([P, WORD_BLOCKS], F32)
+        mean_columns = const.tile([P, WORD_BLOCKS, P], F32)
         x_codes = const.tile([P, FEATURE_PASSES * X_ROWS], U32, align_bytes=64)
         x_scales = const.tile([P, FEATURE_PASSES * X_ROWS], U8, align_bytes=64)
         w_codes = const.tile([P, REF_PASSES * COMPONENTS], U32, align_bytes=64)
         w_scales = const.tile([P, REF_PASSES * COMPONENTS], U8, align_bytes=64)
-        projection = projection_psum.tile([X_ROWS, COMPONENTS], F32)
+        kernel_codes = const.tile([P, REF_PASSES * X_ROWS], U32, align_bytes=64)
+        kernel_scales = const.tile([P, REF_PASSES * X_ROWS], U8, align_bytes=64)
 
         nc.vector.memset(w_scales[:].bitcast(I32), 0)
 
@@ -93,17 +107,46 @@ def tile_quantumkernelpca_w_kernel(
                     .bitcast(I32),
                 )
 
+        def spread_mean_words():
+            bank = transpose_psum.tile([P, BANK_PASSES, PAIR, P], F32)
+            nc.tensor.transpose(bank[:, 0, 0, :], mean_rows[:].bitcast(F32), identity[:])
+            nc.vector.tensor_copy(out=mean_words[:], in_=bank[:, 0, 0, :WORD_BLOCKS])
+
+        def widen_mean(c):
+            blocks = slice(c * CHUNK_BLOCKS, (c + 1) * CHUNK_BLOCKS)
+            copy = nc.vector.tensor_copy if c == 0 else nc.scalar.copy
+            copy(
+                out=mean_columns[:, blocks, :],
+                in_=mean_words[:, blocks].unsqueeze(2).to_broadcast([P, CHUNK_BLOCKS, P]),
+            )
+
+        mean_banks = {}
+
+        def fill_mean(k):
+            bank = mean_psum.tile([P, HALF_BLOCKS, P], F32)
+            first = k % (FEATURES // HALF) * HALF_BLOCKS
+            for b in range(HALF_BLOCKS):
+                nc.tensor.transpose(bank[:, b, :], mean_columns[:, first + b, :], identity[:])
+            mean_banks[k] = bank
+
         def centre_and_square(i, c):
             cols = slice(c * CHUNK, (c + 1) * CHUNK)
             if c == 0:
                 centred = centred_pool.tile([P, FEATURES], F32)
                 sums = stat_pool.tile([P, CHUNKS], F32)
                 work[i] = {"centred": centred, "sums": sums, "grouped": {}}
-            if i == 0:
-                nc.sync.dma_start(out=mean_all[:, cols], in_=mean_[cols].partition_broadcast(P))
             raw = raw_pool.tile([P, CHUNK], BF16)
             nc.sync.dma_start(out=raw[:], in_=row_tiles[i][:, cols])
-            nc.vector.tensor_sub(out=work[i]["centred"][:, cols], in0=raw[:], in1=mean_all[:, cols])
+            for h in range(HALVES):
+                k = (i * CHUNKS + c) * HALVES + h
+                if k + MEAN_BANKS - 1 < ROW_TILES * CHUNKS * HALVES:
+                    fill_mean(k + MEAN_BANKS - 1)
+                bank = mean_banks.pop(k)
+                nc.vector.tensor_sub(
+                    out=work[i]["centred"][:, c * CHUNK + h * HALF : c * CHUNK + (h + 1) * HALF],
+                    in0=raw[:, h * HALF : (h + 1) * HALF],
+                    in1=bank[:].rearrange("p b r -> p (b r)").bitcast(BF16),
+                )
             squares = squares_pool.tile([P, CHUNK], BF16)
             nc.scalar.activation(
                 out=squares[:],
@@ -129,18 +172,15 @@ def tile_quantumkernelpca_w_kernel(
                 nc.vector.reciprocal(out=inverse[:], in_=inverse[:])
                 work[i]["inverse"] = inverse
             unit = unit_pool.tile([P, CHUNK], BF16)
-            split = c * CHUNK + VECTOR_COLUMNS
-            nc.vector.tensor_scalar_mul(
-                out=unit[:, :VECTOR_COLUMNS],
-                in0=work[i]["centred"][:, c * CHUNK : split],
-                scalar1=work[i]["inverse"][:, 0:1],
-            )
-            nc.scalar.activation(
-                out=unit[:, VECTOR_COLUMNS:],
-                in_=work[i]["centred"][:, split : (c + 1) * CHUNK],
-                func=ACT.Copy,
-                scale=work[i]["inverse"][:, 0:1],
-            )
+            for start in range(0, CHUNK, SCALE_COLUMNS):
+                nc.gpsimd.tensor_scalar(
+                    out=unit[:, start : start + SCALE_COLUMNS],
+                    in0=work[i]["centred"][:, c * CHUNK + start : c * CHUNK + start + SCALE_COLUMNS],
+                    scalar1=work[i]["inverse"][:, 0:1],
+                    scalar2=0.0,
+                    op0=ALU.mult,
+                    op1=ALU.add,
+                )
             unit_words = unit[:].bitcast(F32)
             grouped = grouped_pool.tile([P, CHUNK], BF16, align_bytes=64)
             grouped_words = grouped[:].bitcast(F32).rearrange(
@@ -154,7 +194,9 @@ def tile_quantumkernelpca_w_kernel(
                         nc.tensor.transpose(
                             bank[:, g, u, :], unit_words[:, start : start + P], identity[:]
                         )
-                nc.scalar.copy(
+                on_vector = c % 2 == 1 and first > 0
+                copy = nc.vector.tensor_copy if on_vector else nc.scalar.copy
+                copy(
                     out=grouped_words[:, first : first + BANK_PASSES],
                     in_=bank[:].rearrange("p g u r -> p g r u"),
                 )
@@ -199,29 +241,24 @@ def tile_quantumkernelpca_w_kernel(
                 out=work["kernel", g][:, :, t], in_=work[i]["overlap"][:], func=ACT.Square
             )
 
-        def project(g):
-            kernel_codes = kernel_pool.tile([P, X_ROWS], U32, align_bytes=64)
-            kernel_scales = kernel_pool.tile([P, X_ROWS], U8, align_bytes=64)
+        def quantise_kernel(g):
+            words = slice(g * X_ROWS, (g + 1) * X_ROWS)
             nc.vector.quantize_mx(
-                out=kernel_codes[:].bitcast(FP8X4),
-                scales=kernel_scales[:],
+                out=kernel_codes[:, words].bitcast(FP8X4),
+                scales=kernel_scales[:, words],
                 in_=work["kernel", g][:].rearrange("p n t -> p (n t)"),
-            )
-            pass_words = slice(g * COMPONENTS, (g + 1) * COMPONENTS)
-            nc.tensor.matmul_mx(
-                out=projection[:],
-                lhsT=kernel_codes[:].bitcast(FP8X4),
-                lhsT_scale=kernel_scales[:],
-                rhs=w_codes[:, pass_words].bitcast(FP8X4),
-                rhs_scale=w_scales[:, pass_words],
-                start=(g == 0),
-                stop=(g == REF_PASSES - 1),
             )
 
         chunks = [(i, c) for i in range(ROW_TILES) for c in range(CHUNKS)]
+        spread_mean_words()
+        widen_mean(0)
+        for k in range(MEAN_BANKS - 1):
+            fill_mean(k)
         for step in range(len(chunks) + PROJECT_LAG):
             if step < len(chunks):
                 i, c = chunks[step]
+                if step + 1 < CHUNKS:
+                    widen_mean(step + 1)
                 centre_and_square(i, c)
                 if c == CHUNKS - 1:
                     row_norm(i)
@@ -238,8 +275,20 @@ def tile_quantumkernelpca_w_kernel(
             if 0 <= step - PROJECT_LAG < len(chunks):
                 i, c = chunks[step - PROJECT_LAG]
                 if i > 0 and i % PACK == 0 and c == CHUNKS - 1:
-                    project(i // PACK - 1)
+                    quantise_kernel(i // PACK - 1)
 
+        overlap = overlap_psum.tile([X_ROWS, COMPONENTS], F32)
+        for g in range(REF_PASSES):
+            words = slice(g * X_ROWS, (g + 1) * X_ROWS)
+            nc.tensor.matmul_mx(
+                out=overlap[:],
+                lhsT=kernel_codes[:, words].bitcast(FP8X4),
+                lhsT_scale=kernel_scales[:, words],
+                rhs=w_codes[:, words].bitcast(FP8X4),
+                rhs_scale=w_scales[:, words],
+                start=(g == 0),
+                stop=(g == REF_PASSES - 1),
+            )
         result = const.tile([X_ROWS, COMPONENTS], F32)
-        nc.vector.tensor_copy(out=result[:], in_=projection[:])
+        nc.vector.tensor_copy(out=result[:], in_=overlap[:])
         nc.sync.dma_start(out=out, in_=result[:])

@@ -39,7 +39,7 @@ HALVES = CHUNK // HALF
 HALF_BLOCKS = HALF // (PAIR * P)
 CHUNK_BLOCKS = CHUNK // (PAIR * P)
 MEAN_BANKS = 3
-SCALE_COLUMNS = 1024
+GPSIMD_COLUMNS = 1024
 
 CENTRED_TILES = 3
 NORMALISE_LAG = (CENTRED_TILES - 1) * CHUNKS
@@ -172,15 +172,20 @@ def tile_quantumkernelpca_w_kernel(
                 nc.vector.reciprocal(out=inverse[:], in_=inverse[:])
                 work[i]["inverse"] = inverse
             unit = unit_pool.tile([P, CHUNK], BF16)
-            for start in range(0, CHUNK, SCALE_COLUMNS):
-                nc.gpsimd.tensor_scalar(
-                    out=unit[:, start : start + SCALE_COLUMNS],
-                    in0=work[i]["centred"][:, c * CHUNK + start : c * CHUNK + start + SCALE_COLUMNS],
-                    scalar1=work[i]["inverse"][:, 0:1],
-                    scalar2=0.0,
-                    op0=ALU.mult,
-                    op1=ALU.add,
-                )
+            split = c * CHUNK + GPSIMD_COLUMNS
+            nc.gpsimd.tensor_scalar(
+                out=unit[:, :GPSIMD_COLUMNS],
+                in0=work[i]["centred"][:, c * CHUNK : split],
+                scalar1=work[i]["inverse"][:, 0:1],
+                scalar2=0.0,
+                op0=ALU.mult,
+                op1=ALU.add,
+            )
+            nc.vector.tensor_scalar_mul(
+                out=unit[:, GPSIMD_COLUMNS:],
+                in0=work[i]["centred"][:, split : (c + 1) * CHUNK],
+                scalar1=work[i]["inverse"][:, 0:1],
+            )
             unit_words = unit[:].bitcast(F32)
             grouped = grouped_pool.tile([P, CHUNK], BF16, align_bytes=64)
             grouped_words = grouped[:].bitcast(F32).rearrange(
@@ -194,9 +199,7 @@ def tile_quantumkernelpca_w_kernel(
                         nc.tensor.transpose(
                             bank[:, g, u, :], unit_words[:, start : start + P], identity[:]
                         )
-                on_vector = c % 2 == 1 and first > 0
-                copy = nc.vector.tensor_copy if on_vector else nc.scalar.copy
-                copy(
+                nc.scalar.copy(
                     out=grouped_words[:, first : first + BANK_PASSES],
                     in_=bank[:].rearrange("p g u r -> p g r u"),
                 )

@@ -31,20 +31,23 @@ CHUNKS = FEATURES // CHUNK
 CHUNK_PASSES = CHUNK // K_PASS
 PAIR = 2
 BANK_PASSES = 2
-
-WORDS = FEATURES // PAIR
-WORD_BLOCKS = WORDS // P
+WORD_BLOCKS = FEATURES // PAIR // P
 HALF = PAIR * 512
 HALVES = CHUNK // HALF
 HALF_BLOCKS = HALF // (PAIR * P)
 CHUNK_BLOCKS = CHUNK // (PAIR * P)
-MEAN_BANKS = 3
+
 GPSIMD_COLUMNS = 1024
 
-CENTRED_TILES = 3
-NORMALISE_LAG = (CENTRED_TILES - 1) * CHUNKS
-QUANTISE_LAG = NORMALISE_LAG + 1
-PROJECT_LAG = QUANTISE_LAG + 1
+SQUARE_LAG = 1
+INVERT_LAG = 2
+SCALE_LAG = 6
+TRANSPOSE_LAG = 7
+GROUP_LAG = 8
+QUANTISE_LAG = 9
+OVERLAP_LAG = 10
+KERNEL_LAG = 11
+LOAD_AHEAD = 6
 
 FLOPS = 2 * X_ROWS * REF_ROWS * FEATURES + 2 * X_ROWS * REF_ROWS * COMPONENTS
 
@@ -59,16 +62,16 @@ def tile_quantumkernelpca_w_kernel(
 
     with ExitStack() as ctx:
         const = ctx.enter_context(tc.tile_pool(name="const", bufs=1))
-        raw_pool = ctx.enter_context(tc.tile_pool(name="raw", bufs=8))
-        centred_pool = ctx.enter_context(tc.tile_pool(name="centred", bufs=CENTRED_TILES))
+        raw_pool = ctx.enter_context(tc.tile_pool(name="raw", bufs=LOAD_AHEAD + 2))
+        centred_pool = ctx.enter_context(tc.tile_pool(name="centred", bufs=SCALE_LAG + 2))
         squares_pool = ctx.enter_context(tc.tile_pool(name="squares", bufs=2))
-        stat_pool = ctx.enter_context(tc.tile_pool(name="stat", bufs=3))
+        stat_pool = ctx.enter_context(tc.tile_pool(name="stat", bufs=4))
         unit_pool = ctx.enter_context(tc.tile_pool(name="unit", bufs=3))
         grouped_pool = ctx.enter_context(tc.tile_pool(name="grouped", bufs=3))
         codes_pool = ctx.enter_context(tc.tile_pool(name="codes", bufs=2))
         kernel_pool = ctx.enter_context(tc.tile_pool(name="kernel", bufs=2))
         transpose_psum = ctx.enter_context(tc.psum_pool(name="transpose_psum", bufs=3))
-        mean_psum = ctx.enter_context(tc.psum_pool(name="mean_psum", bufs=MEAN_BANKS))
+        mean_psum = ctx.enter_context(tc.psum_pool(name="mean_psum", bufs=3))
         overlap_psum = ctx.enter_context(tc.psum_pool(name="overlap_psum", bufs=2))
 
         mean_rows = const.tile([P, PAIR * P], BF16)
@@ -90,7 +93,9 @@ def tile_quantumkernelpca_w_kernel(
 
         nc.vector.memset(w_scales[:].bitcast(I32), 0)
 
-        work = {}
+        chunks = [(i, c) for i in range(ROW_TILES) for c in range(CHUNKS)]
+        raws, mean_banks, centreds, units, transposed, groupeds = {}, {}, {}, {}, {}, {}
+        sums, norms, inverses, codes_of, overlaps, kernels = {}, {}, {}, {}, {}, {}
 
         def load_weight():
             nc.sync.dma_start(
@@ -107,90 +112,94 @@ def tile_quantumkernelpca_w_kernel(
                     .bitcast(I32),
                 )
 
+        def load(n):
+            i, c = chunks[n]
+            raw = raw_pool.tile([P, CHUNK], BF16)
+            nc.sync.dma_start(out=raw[:], in_=row_tiles[i][:, c * CHUNK : (c + 1) * CHUNK])
+            raws[n] = raw
+
         def spread_mean_words():
             bank = transpose_psum.tile([P, BANK_PASSES, PAIR, P], F32)
             nc.tensor.transpose(bank[:, 0, 0, :], mean_rows[:].bitcast(F32), identity[:])
             nc.vector.tensor_copy(out=mean_words[:], in_=bank[:, 0, 0, :WORD_BLOCKS])
 
-        def widen_mean(c):
+        def widen_mean(c, copy):
             blocks = slice(c * CHUNK_BLOCKS, (c + 1) * CHUNK_BLOCKS)
-            copy = nc.vector.tensor_copy if c == 0 else nc.scalar.copy
             copy(
                 out=mean_columns[:, blocks, :],
                 in_=mean_words[:, blocks].unsqueeze(2).to_broadcast([P, CHUNK_BLOCKS, P]),
             )
 
-        mean_banks = {}
-
-        def fill_mean(k):
+        def fill_mean(n, h):
+            c = chunks[n][1]
             bank = mean_psum.tile([P, HALF_BLOCKS, P], F32)
-            first = k % (FEATURES // HALF) * HALF_BLOCKS
             for b in range(HALF_BLOCKS):
-                nc.tensor.transpose(bank[:, b, :], mean_columns[:, first + b, :], identity[:])
-            mean_banks[k] = bank
+                block = (c * HALVES + h) * HALF_BLOCKS + b
+                nc.tensor.transpose(bank[:, b, :], mean_columns[:, block, :], identity[:])
+            mean_banks[n, h] = bank
 
-        def centre_and_square(i, c):
-            cols = slice(c * CHUNK, (c + 1) * CHUNK)
+        def centre(n, h):
+            if h == 0:
+                centred = centred_pool.tile([P, CHUNK], F32)
+                centreds[n] = centred
+            cols = slice(h * HALF, (h + 1) * HALF)
+            nc.vector.tensor_sub(
+                out=centreds[n][:, cols],
+                in0=raws[n][:, cols],
+                in1=mean_banks.pop((n, h))[:].rearrange("p b r -> p (b r)").bitcast(BF16),
+            )
+
+        def square(n):
+            i, c = chunks[n]
             if c == 0:
-                centred = centred_pool.tile([P, FEATURES], F32)
-                sums = stat_pool.tile([P, CHUNKS], F32)
-                work[i] = {"centred": centred, "sums": sums, "grouped": {}}
-            raw = raw_pool.tile([P, CHUNK], BF16)
-            nc.sync.dma_start(out=raw[:], in_=row_tiles[i][:, cols])
-            for h in range(HALVES):
-                k = (i * CHUNKS + c) * HALVES + h
-                if k + MEAN_BANKS - 1 < ROW_TILES * CHUNKS * HALVES:
-                    fill_mean(k + MEAN_BANKS - 1)
-                bank = mean_banks.pop(k)
-                nc.vector.tensor_sub(
-                    out=work[i]["centred"][:, c * CHUNK + h * HALF : c * CHUNK + (h + 1) * HALF],
-                    in0=raw[:, h * HALF : (h + 1) * HALF],
-                    in1=bank[:].rearrange("p b r -> p (b r)").bitcast(BF16),
-                )
+                tile_sums = stat_pool.tile([P, CHUNKS], F32)
+                sums[i] = tile_sums
             squares = squares_pool.tile([P, CHUNK], BF16)
             nc.scalar.activation(
                 out=squares[:],
-                in_=work[i]["centred"][:, cols],
+                in_=centreds[n][:],
                 func=ACT.Square,
-                accum_out=work[i]["sums"][:, c : c + 1],
+                accum_out=sums[i][:, c : c + 1],
             )
+            if c == CHUNKS - 1:
+                sums_again = stat_pool.tile([P, CHUNKS], F32)
+                total = stat_pool.tile([P, 1], F32)
+                nc.scalar.activation(
+                    out=sums_again[:], in_=sums[i][:], func=ACT.Copy, accum_out=total[:]
+                )
+                norm = stat_pool.tile([P, 1], F32)
+                nc.scalar.activation(out=norm[:], in_=total[:], func=ACT.Sqrt)
+                norms[i] = norm
 
-        def row_norm(i):
-            sums_again = stat_pool.tile([P, CHUNKS], F32)
-            total = stat_pool.tile([P, 1], F32)
-            nc.scalar.activation(
-                out=sums_again[:], in_=work[i]["sums"][:], func=ACT.Copy, accum_out=total[:]
-            )
-            norm = stat_pool.tile([P, 1], F32)
-            nc.scalar.activation(out=norm[:], in_=total[:], func=ACT.Sqrt)
-            work[i]["norm"] = norm
+        def invert(i):
+            inverse = stat_pool.tile([P, 1], F32)
+            nc.vector.tensor_scalar_add(out=inverse[:], in0=norms[i][:], scalar1=EPS)
+            nc.vector.reciprocal(out=inverse[:], in_=inverse[:])
+            inverses[i] = inverse
 
-        def normalise_and_transpose(i, c):
-            if c == 0:
-                inverse = stat_pool.tile([P, 1], F32)
-                nc.vector.tensor_scalar_add(out=inverse[:], in0=work[i]["norm"][:], scalar1=EPS)
-                nc.vector.reciprocal(out=inverse[:], in_=inverse[:])
-                work[i]["inverse"] = inverse
+        def scale(n):
+            i, c = chunks[n]
             unit = unit_pool.tile([P, CHUNK], BF16)
-            split = c * CHUNK + GPSIMD_COLUMNS
+            nc.vector.tensor_scalar_mul(
+                out=unit[:, GPSIMD_COLUMNS:],
+                in0=centreds[n][:, GPSIMD_COLUMNS:],
+                scalar1=inverses[i][:, 0:1],
+            )
+            factor = stat_pool.tile([P, 1], F32)
+            nc.vector.tensor_copy(out=factor[:], in_=inverses[i][:])
             nc.gpsimd.tensor_scalar(
                 out=unit[:, :GPSIMD_COLUMNS],
-                in0=work[i]["centred"][:, c * CHUNK : split],
-                scalar1=work[i]["inverse"][:, 0:1],
+                in0=centreds[n][:, :GPSIMD_COLUMNS],
+                scalar1=factor[:, 0:1],
                 scalar2=0.0,
                 op0=ALU.mult,
                 op1=ALU.add,
             )
-            nc.vector.tensor_scalar_mul(
-                out=unit[:, GPSIMD_COLUMNS:],
-                in0=work[i]["centred"][:, split : (c + 1) * CHUNK],
-                scalar1=work[i]["inverse"][:, 0:1],
-            )
-            unit_words = unit[:].bitcast(F32)
-            grouped = grouped_pool.tile([P, CHUNK], BF16, align_bytes=64)
-            grouped_words = grouped[:].bitcast(F32).rearrange(
-                "p (g r u) -> p g r u", g=CHUNK_PASSES, u=PAIR
-            )
+            units[n] = unit
+
+        def transpose(n):
+            unit_words = units.pop(n)[:].bitcast(F32)
+            banks = []
             for first in range(0, CHUNK_PASSES, BANK_PASSES):
                 bank = transpose_psum.tile([P, BANK_PASSES, PAIR, P], F32)
                 for g in range(BANK_PASSES):
@@ -199,38 +208,54 @@ def tile_quantumkernelpca_w_kernel(
                         nc.tensor.transpose(
                             bank[:, g, u, :], unit_words[:, start : start + P], identity[:]
                         )
+                banks.append(bank)
+            transposed[n] = banks
+
+        def group(n):
+            grouped = grouped_pool.tile([P, CHUNK], BF16, align_bytes=64)
+            grouped_words = grouped[:].bitcast(F32).rearrange(
+                "p (g r u) -> p g r u", g=CHUNK_PASSES, u=PAIR
+            )
+            for b, bank in enumerate(transposed.pop(n)):
                 nc.scalar.copy(
-                    out=grouped_words[:, first : first + BANK_PASSES],
+                    out=grouped_words[:, b * BANK_PASSES : (b + 1) * BANK_PASSES],
                     in_=bank[:].rearrange("p g u r -> p g r u"),
                 )
-            work[i]["grouped"][c] = grouped
+            groupeds[n] = grouped
 
-        def quantise_and_multiply(i, c):
+        def quantise(n):
+            i, c = chunks[n]
             if c == 0:
                 if i == 0:
-                    work[i]["codes"], work[i]["scales"] = x_codes, x_scales
+                    codes_of[i] = (x_codes, x_scales)
                 else:
                     codes = codes_pool.tile([P, FEATURE_PASSES * P], U32, align_bytes=64)
                     scales = codes_pool.tile([P, FEATURE_PASSES * P], U8, align_bytes=64)
-                    overlap = overlap_psum.tile([P, X_ROWS], F32)
-                    work[i]["codes"], work[i]["scales"], work[i]["overlap"] = codes, scales, overlap
-            codes, scales = work[i]["codes"], work[i]["scales"]
-            chunk_words = slice(c * CHUNK_PASSES * P, (c + 1) * CHUNK_PASSES * P)
+                    codes_of[i] = (codes, scales)
+            tile_codes, tile_scales = codes_of[i]
+            words = slice(c * CHUNK_PASSES * P, (c + 1) * CHUNK_PASSES * P)
             nc.vector.quantize_mx(
-                out=codes[:, chunk_words].bitcast(FP8X4),
-                scales=scales[:, chunk_words],
-                in_=work[i]["grouped"][c][:],
+                out=tile_codes[:, words].bitcast(FP8X4),
+                scales=tile_scales[:, words],
+                in_=groupeds.pop(n)[:],
             )
+
+        def multiply(n):
+            i, c = chunks[n]
             if i == 0:
                 return
+            if c == 0:
+                overlap = overlap_psum.tile([P, X_ROWS], F32)
+                overlaps[i] = overlap
+            tile_codes, tile_scales = codes_of[i]
             for g in range(c * CHUNK_PASSES, (c + 1) * CHUNK_PASSES):
-                pass_words = slice(g * P, (g + 1) * P)
+                words = slice(g * P, (g + 1) * P)
                 nc.tensor.matmul_mx(
-                    out=work[i]["overlap"][:],
-                    lhsT=codes[:, pass_words].bitcast(FP8X4),
-                    lhsT_scale=scales[:, pass_words],
-                    rhs=x_codes[:, pass_words].bitcast(FP8X4),
-                    rhs_scale=x_scales[:, pass_words],
+                    out=overlaps[i][:],
+                    lhsT=tile_codes[:, words].bitcast(FP8X4),
+                    lhsT_scale=tile_scales[:, words],
+                    rhs=x_codes[:, words].bitcast(FP8X4),
+                    rhs_scale=x_scales[:, words],
                     start=(g == 0),
                     stop=(g == FEATURE_PASSES - 1),
                 )
@@ -239,9 +264,9 @@ def tile_quantumkernelpca_w_kernel(
             g, t = divmod(i - 1, PACK)
             if t == 0:
                 kernel_grouped = kernel_pool.tile([P, X_ROWS, PACK], BF16, align_bytes=64)
-                work["kernel", g] = kernel_grouped
+                kernels[g] = kernel_grouped
             nc.scalar.activation(
-                out=work["kernel", g][:, :, t], in_=work[i]["overlap"][:], func=ACT.Square
+                out=kernels[g][:, :, t], in_=overlaps.pop(i)[:], func=ACT.Square
             )
 
         def quantise_kernel(g):
@@ -249,36 +274,58 @@ def tile_quantumkernelpca_w_kernel(
             nc.vector.quantize_mx(
                 out=kernel_codes[:, words].bitcast(FP8X4),
                 scales=kernel_scales[:, words],
-                in_=work["kernel", g][:].rearrange("p n t -> p (n t)"),
+                in_=kernels.pop(g)[:].rearrange("p n t -> p (n t)"),
             )
 
-        chunks = [(i, c) for i in range(ROW_TILES) for c in range(CHUNKS)]
+        def live(n):
+            return 0 <= n < len(chunks)
+
+        def last_of(n):
+            return n // CHUNKS if live(n) and n % CHUNKS == CHUNKS - 1 else None
+
+        ctx.enter_context(tc.manual_schedule())
+        for n in range(LOAD_AHEAD):
+            load(n)
         spread_mean_words()
-        widen_mean(0)
-        for k in range(MEAN_BANKS - 1):
-            fill_mean(k)
-        for step in range(len(chunks) + PROJECT_LAG):
-            if step < len(chunks):
-                i, c = chunks[step]
-                if step + 1 < CHUNKS:
-                    widen_mean(step + 1)
-                centre_and_square(i, c)
-                if c == CHUNKS - 1:
-                    row_norm(i)
-                if step == CHUNKS:
-                    load_weight()
-            if 0 <= step - NORMALISE_LAG < len(chunks):
-                i, c = chunks[step - NORMALISE_LAG]
-                normalise_and_transpose(i, c)
-            if 0 <= step - QUANTISE_LAG < len(chunks):
-                i, c = chunks[step - QUANTISE_LAG]
-                quantise_and_multiply(i, c)
-                if i > 0 and c == CHUNKS - 1:
-                    square_overlaps(i)
-            if 0 <= step - PROJECT_LAG < len(chunks):
-                i, c = chunks[step - PROJECT_LAG]
-                if i > 0 and i % PACK == 0 and c == CHUNKS - 1:
-                    quantise_kernel(i // PACK - 1)
+        widen_mean(0, nc.vector.tensor_copy)
+        fill_mean(0, 0)
+        fill_mean(0, 1)
+        for step in range(len(chunks) + KERNEL_LAG + 1):
+            if live(step + LOAD_AHEAD):
+                load(step + LOAD_AHEAD)
+            if step == 1:
+                load_weight()
+            if step + 1 < CHUNKS:
+                widen_mean(step + 1, nc.scalar.copy)
+
+            if live(step - GROUP_LAG):
+                group(step - GROUP_LAG)
+            if live(step - TRANSPOSE_LAG):
+                transpose(step - TRANSPOSE_LAG)
+            if live(step + 1):
+                fill_mean(step + 1, 0)
+            if live(step - QUANTISE_LAG):
+                quantise(step - QUANTISE_LAG)
+                multiply(step - QUANTISE_LAG)
+            tile = last_of(step - KERNEL_LAG)
+            if tile is not None and tile > 0 and tile % PACK == 0:
+                quantise_kernel(tile // PACK - 1)
+            tile = last_of(step - INVERT_LAG)
+            if tile is not None:
+                invert(tile)
+            if live(step - SCALE_LAG):
+                scale(step - SCALE_LAG)
+            if live(step):
+                centre(step, 0)
+            if live(step + 1):
+                fill_mean(step + 1, 1)
+            if live(step):
+                centre(step, 1)
+            if live(step - SQUARE_LAG):
+                square(step - SQUARE_LAG)
+            tile = last_of(step - OVERLAP_LAG)
+            if tile is not None and tile > 0:
+                square_overlaps(tile)
 
         overlap = overlap_psum.tile([X_ROWS, COMPONENTS], F32)
         for g in range(REF_PASSES):

@@ -37,7 +37,8 @@ HALVES = CHUNK // HALF
 HALF_BLOCKS = HALF // (PAIR * P)
 CHUNK_BLOCKS = CHUNK // (PAIR * P)
 
-GPSIMD_COLUMNS = 1024
+VECTOR_SHARE = 1536
+VECTOR_COPIES = 2
 
 SQUARE_LAG = 1
 INVERT_LAG = 2
@@ -66,13 +67,13 @@ def tile_quantumkernelpca_w_kernel(
         centred_pool = ctx.enter_context(tc.tile_pool(name="centred", bufs=SCALE_LAG + 2))
         squares_pool = ctx.enter_context(tc.tile_pool(name="squares", bufs=2))
         stat_pool = ctx.enter_context(tc.tile_pool(name="stat", bufs=4))
-        unit_pool = ctx.enter_context(tc.tile_pool(name="unit", bufs=3))
-        grouped_pool = ctx.enter_context(tc.tile_pool(name="grouped", bufs=3))
+        stage_pool = ctx.enter_context(tc.tile_pool(name="stage", bufs=3))
         codes_pool = ctx.enter_context(tc.tile_pool(name="codes", bufs=2))
         kernel_pool = ctx.enter_context(tc.tile_pool(name="kernel", bufs=2))
-        transpose_psum = ctx.enter_context(tc.psum_pool(name="transpose_psum", bufs=3))
-        mean_psum = ctx.enter_context(tc.psum_pool(name="mean_psum", bufs=3))
-        overlap_psum = ctx.enter_context(tc.psum_pool(name="overlap_psum", bufs=2))
+        static_psum = ctx.enter_context(tc.psum_pool(name="static_psum", bufs=1))
+        transpose_psum = ctx.enter_context(tc.psum_pool(name="transpose_psum", bufs=2))
+        mean_psum = ctx.enter_context(tc.psum_pool(name="mean_psum", bufs=1))
+        overlap_psum = ctx.enter_context(tc.psum_pool(name="overlap_psum", bufs=1))
 
         mean_rows = const.tile([P, PAIR * P], BF16)
         nc.vector.memset(mean_rows[:], 0.0)
@@ -92,6 +93,10 @@ def tile_quantumkernelpca_w_kernel(
         kernel_scales = const.tile([P, REF_PASSES * X_ROWS], U8, align_bytes=64)
 
         nc.vector.memset(w_scales[:].bitcast(I32), 0)
+
+        warm = const.tile([P, 1], F32)
+        nc.vector.memset(warm[:], 0.0)
+        nc.scalar.activation(out=warm[:], in_=warm[:], func=ACT.Sqrt)
 
         chunks = [(i, c) for i in range(ROW_TILES) for c in range(CHUNKS)]
         raws, mean_banks, centreds, units, transposed, groupeds = {}, {}, {}, {}, {}, {}
@@ -123,20 +128,22 @@ def tile_quantumkernelpca_w_kernel(
             nc.tensor.transpose(bank[:, 0, 0, :], mean_rows[:].bitcast(F32), identity[:])
             nc.vector.tensor_copy(out=mean_words[:], in_=bank[:, 0, 0, :WORD_BLOCKS])
 
-        def widen_mean(c, copy):
+        def widen_mean(c):
             blocks = slice(c * CHUNK_BLOCKS, (c + 1) * CHUNK_BLOCKS)
-            copy(
+            nc.vector.tensor_copy(
                 out=mean_columns[:, blocks, :],
                 in_=mean_words[:, blocks].unsqueeze(2).to_broadcast([P, CHUNK_BLOCKS, P]),
             )
 
-        def fill_mean(n, h):
-            c = chunks[n][1]
-            bank = mean_psum.tile([P, HALF_BLOCKS, P], F32)
+        def fill_mean(c, h):
+            if h == 0:
+                bank = static_psum.tile([P, HALF_BLOCKS, P], F32, name="static_%d" % c)
+            else:
+                bank = mean_psum.tile([P, HALF_BLOCKS, P], F32, name="mean_bank")
             for b in range(HALF_BLOCKS):
                 block = (c * HALVES + h) * HALF_BLOCKS + b
                 nc.tensor.transpose(bank[:, b, :], mean_columns[:, block, :], identity[:])
-            mean_banks[n, h] = bank
+            mean_banks[c, h] = bank
 
         def centre(n, h):
             if h == 0:
@@ -146,7 +153,7 @@ def tile_quantumkernelpca_w_kernel(
             nc.vector.tensor_sub(
                 out=centreds[n][:, cols],
                 in0=raws[n][:, cols],
-                in1=mean_banks.pop((n, h))[:].rearrange("p b r -> p (b r)").bitcast(BF16),
+                in1=mean_banks[chunks[n][1], h][:].rearrange("p b r -> p (b r)").bitcast(BF16),
             )
 
         def square(n):
@@ -177,24 +184,30 @@ def tile_quantumkernelpca_w_kernel(
             nc.vector.reciprocal(out=inverse[:], in_=inverse[:])
             inverses[i] = inverse
 
-        def scale(n):
+        def scale(n, subtracting):
             i, c = chunks[n]
-            unit = unit_pool.tile([P, CHUNK], BF16)
-            nc.vector.tensor_scalar_mul(
-                out=unit[:, GPSIMD_COLUMNS:],
-                in0=centreds[n][:, GPSIMD_COLUMNS:],
-                scalar1=inverses[i][:, 0:1],
-            )
-            factor = stat_pool.tile([P, 1], F32)
-            nc.vector.tensor_copy(out=factor[:], in_=inverses[i][:])
-            nc.gpsimd.tensor_scalar(
-                out=unit[:, :GPSIMD_COLUMNS],
-                in0=centreds[n][:, :GPSIMD_COLUMNS],
-                scalar1=factor[:, 0:1],
-                scalar2=0.0,
-                op0=ALU.mult,
-                op1=ALU.add,
-            )
+            unit = stage_pool.tile([P, CHUNK], BF16, align_bytes=64, name="stage")
+            if subtracting:
+                nc.gpsimd.tensor_scalar(
+                    out=unit[:],
+                    in0=centreds[n][:],
+                    scalar1=inverses[i][:, 0:1],
+                    scalar2=0.0,
+                    op0=ALU.mult,
+                    op1=ALU.add,
+                )
+            else:
+                nc.vector.tensor_scalar_mul(
+                    out=unit[:, :VECTOR_SHARE],
+                    in0=centreds[n][:, :VECTOR_SHARE],
+                    scalar1=inverses[i][:, 0:1],
+                )
+                nc.scalar.activation(
+                    out=unit[:, VECTOR_SHARE:],
+                    in_=centreds[n][:, VECTOR_SHARE:],
+                    func=ACT.Copy,
+                    scale=inverses[i][:, 0:1],
+                )
             units[n] = unit
 
         def transpose(n):
@@ -212,12 +225,14 @@ def tile_quantumkernelpca_w_kernel(
             transposed[n] = banks
 
         def group(n):
-            grouped = grouped_pool.tile([P, CHUNK], BF16, align_bytes=64)
+            grouped = stage_pool.tile([P, CHUNK], BF16, align_bytes=64, name="stage")
             grouped_words = grouped[:].bitcast(F32).rearrange(
                 "p (g r u) -> p g r u", g=CHUNK_PASSES, u=PAIR
             )
             for b, bank in enumerate(transposed.pop(n)):
-                nc.scalar.copy(
+                by_vector = n % VECTOR_COPIES == 0 and b > 0
+                copy = nc.vector.tensor_copy if by_vector else nc.scalar.copy
+                copy(
                     out=grouped_words[:, b * BANK_PASSES : (b + 1) * BANK_PASSES],
                     in_=bank[:].rearrange("p g u r -> p g r u"),
                 )
@@ -244,14 +259,15 @@ def tile_quantumkernelpca_w_kernel(
             i, c = chunks[n]
             if i == 0:
                 return
-            if c == 0:
-                overlap = overlap_psum.tile([P, X_ROWS], F32)
-                overlaps[i] = overlap
+            group_of_i, t = divmod(i - 1, PACK)
+            if c == 0 and t == 0:
+                overlap = overlap_psum.tile([P, PACK, X_ROWS], F32)
+                overlaps[group_of_i] = overlap
             tile_codes, tile_scales = codes_of[i]
             for g in range(c * CHUNK_PASSES, (c + 1) * CHUNK_PASSES):
                 words = slice(g * P, (g + 1) * P)
                 nc.tensor.matmul_mx(
-                    out=overlaps[i][:],
+                    out=overlaps[group_of_i][:, t, :],
                     lhsT=tile_codes[:, words].bitcast(FP8X4),
                     lhsT_scale=tile_scales[:, words],
                     rhs=x_codes[:, words].bitcast(FP8X4),
@@ -260,14 +276,14 @@ def tile_quantumkernelpca_w_kernel(
                     stop=(g == FEATURE_PASSES - 1),
                 )
 
-        def square_overlaps(i):
-            g, t = divmod(i - 1, PACK)
-            if t == 0:
-                kernel_grouped = kernel_pool.tile([P, X_ROWS, PACK], BF16, align_bytes=64)
-                kernels[g] = kernel_grouped
+        def square_overlaps(g):
+            kernel_grouped = kernel_pool.tile([P, X_ROWS, PACK], BF16, align_bytes=64)
             nc.scalar.activation(
-                out=kernels[g][:, :, t], in_=overlaps.pop(i)[:], func=ACT.Square
+                out=kernel_grouped[:],
+                in_=overlaps.pop(g)[:].rearrange("p t n -> p n t"),
+                func=ACT.Square,
             )
+            kernels[g] = kernel_grouped
 
         def quantise_kernel(g):
             words = slice(g * X_ROWS, (g + 1) * X_ROWS)
@@ -287,25 +303,26 @@ def tile_quantumkernelpca_w_kernel(
         for n in range(LOAD_AHEAD):
             load(n)
         spread_mean_words()
-        widen_mean(0, nc.vector.tensor_copy)
+        widen_mean(0)
         fill_mean(0, 0)
-        fill_mean(0, 1)
         for step in range(len(chunks) + KERNEL_LAG + 1):
             if live(step + LOAD_AHEAD):
                 load(step + LOAD_AHEAD)
             if step == 1:
                 load_weight()
-            if step + 1 < CHUNKS:
-                widen_mean(step + 1, nc.scalar.copy)
 
+            if live(step):
+                fill_mean(chunks[step][1], 1)
+            if live(step - QUANTISE_LAG):
+                quantise(step - QUANTISE_LAG)
             if live(step - GROUP_LAG):
                 group(step - GROUP_LAG)
             if live(step - TRANSPOSE_LAG):
                 transpose(step - TRANSPOSE_LAG)
-            if live(step + 1):
-                fill_mean(step + 1, 0)
+            tile = last_of(step - OVERLAP_LAG)
+            if tile is not None and tile > 0 and tile % PACK == 0:
+                square_overlaps(tile // PACK - 1)
             if live(step - QUANTISE_LAG):
-                quantise(step - QUANTISE_LAG)
                 multiply(step - QUANTISE_LAG)
             tile = last_of(step - KERNEL_LAG)
             if tile is not None and tile > 0 and tile % PACK == 0:
@@ -314,24 +331,22 @@ def tile_quantumkernelpca_w_kernel(
             if tile is not None:
                 invert(tile)
             if live(step - SCALE_LAG):
-                scale(step - SCALE_LAG)
+                scale(step - SCALE_LAG, live(step))
             if live(step):
                 centre(step, 0)
-            if live(step + 1):
-                fill_mean(step + 1, 1)
-            if live(step):
                 centre(step, 1)
+            if step + 1 < CHUNKS:
+                widen_mean(step + 1)
+                fill_mean(step + 1, 0)
             if live(step - SQUARE_LAG):
                 square(step - SQUARE_LAG)
-            tile = last_of(step - OVERLAP_LAG)
-            if tile is not None and tile > 0:
-                square_overlaps(tile)
 
-        overlap = overlap_psum.tile([X_ROWS, COMPONENTS], F32)
+        bank = transpose_psum.tile([P, BANK_PASSES, PAIR, P], F32)
+        overlap = bank[:, 0, 0, :]
         for g in range(REF_PASSES):
             words = slice(g * X_ROWS, (g + 1) * X_ROWS)
             nc.tensor.matmul_mx(
-                out=overlap[:],
+                out=overlap,
                 lhsT=kernel_codes[:, words].bitcast(FP8X4),
                 lhsT_scale=kernel_scales[:, words],
                 rhs=w_codes[:, words].bitcast(FP8X4),
@@ -340,5 +355,5 @@ def tile_quantumkernelpca_w_kernel(
                 stop=(g == REF_PASSES - 1),
             )
         result = const.tile([X_ROWS, COMPONENTS], F32)
-        nc.vector.tensor_copy(out=result[:], in_=overlap[:])
+        nc.vector.tensor_copy(out=result[:], in_=overlap)
         nc.sync.dma_start(out=out, in_=result[:])

@@ -37,17 +37,18 @@ HALVES = CHUNK // HALF
 HALF_BLOCKS = HALF // (PAIR * P)
 CHUNK_BLOCKS = CHUNK // (PAIR * P)
 
-VECTOR_SHARE = 1536
+GPSIMD_COLUMNS = 1984
+OVERLAP_COLUMNS = 16
 VECTOR_COPIES = 2
 
 SQUARE_LAG = 1
-INVERT_LAG = 2
+NORM_LAG = 2
 SCALE_LAG = 6
 TRANSPOSE_LAG = 7
 GROUP_LAG = 8
 QUANTISE_LAG = 9
 OVERLAP_LAG = 10
-KERNEL_LAG = 11
+KERNEL_LAG = 13
 LOAD_AHEAD = 6
 
 FLOPS = 2 * X_ROWS * REF_ROWS * FEATURES + 2 * X_ROWS * REF_ROWS * COMPONENTS
@@ -67,7 +68,8 @@ def tile_quantumkernelpca_w_kernel(
         centred_pool = ctx.enter_context(tc.tile_pool(name="centred", bufs=SCALE_LAG + 2))
         squares_pool = ctx.enter_context(tc.tile_pool(name="squares", bufs=2))
         stat_pool = ctx.enter_context(tc.tile_pool(name="stat", bufs=4))
-        stage_pool = ctx.enter_context(tc.tile_pool(name="stage", bufs=3))
+        unit_pool = ctx.enter_context(tc.tile_pool(name="unit", bufs=3))
+        grouped_pool = ctx.enter_context(tc.tile_pool(name="grouped", bufs=3))
         codes_pool = ctx.enter_context(tc.tile_pool(name="codes", bufs=2))
         kernel_pool = ctx.enter_context(tc.tile_pool(name="kernel", bufs=2))
         static_psum = ctx.enter_context(tc.psum_pool(name="static_psum", bufs=1))
@@ -100,6 +102,7 @@ def tile_quantumkernelpca_w_kernel(
 
         chunks = [(i, c) for i in range(ROW_TILES) for c in range(CHUNKS)]
         raws, mean_banks, centreds, units, transposed, groupeds = {}, {}, {}, {}, {}, {}
+        totals, divisors = {}, {}
         sums, norms, inverses, codes_of, overlaps, kernels = {}, {}, {}, {}, {}, {}
 
         def load_weight():
@@ -168,47 +171,49 @@ def tile_quantumkernelpca_w_kernel(
                 func=ACT.Square,
                 accum_out=sums[i][:, c : c + 1],
             )
-            if c == CHUNKS - 1:
-                sums_again = stat_pool.tile([P, CHUNKS], F32)
-                total = stat_pool.tile([P, 1], F32)
-                nc.scalar.activation(
-                    out=sums_again[:], in_=sums[i][:], func=ACT.Copy, accum_out=total[:]
-                )
-                norm = stat_pool.tile([P, 1], F32)
-                nc.scalar.activation(out=norm[:], in_=total[:], func=ACT.Sqrt)
-                norms[i] = norm
+
+        def add_sums(i):
+            sums_again = stat_pool.tile([P, CHUNKS], F32)
+            total = stat_pool.tile([P, 1], F32)
+            nc.scalar.activation(
+                out=sums_again[:], in_=sums[i][:], func=ACT.Copy, accum_out=total[:]
+            )
+            totals[i] = total
+
+        def root(i):
+            norm = stat_pool.tile([P, 1], F32)
+            nc.scalar.activation(out=norm[:], in_=totals[i][:], func=ACT.Sqrt)
+            norms[i] = norm
+
+        def add_eps(i):
+            divisor = stat_pool.tile([P, 1], F32)
+            nc.vector.tensor_scalar_add(out=divisor[:], in0=norms[i][:], scalar1=EPS)
+            divisors[i] = divisor
 
         def invert(i):
             inverse = stat_pool.tile([P, 1], F32)
-            nc.vector.tensor_scalar_add(out=inverse[:], in0=norms[i][:], scalar1=EPS)
-            nc.vector.reciprocal(out=inverse[:], in_=inverse[:])
+            nc.vector.reciprocal(out=inverse[:], in_=divisors[i][:])
             inverses[i] = inverse
 
-        def scale(n, subtracting):
-            i, c = chunks[n]
-            unit = stage_pool.tile([P, CHUNK], BF16, align_bytes=64, name="stage")
-            if subtracting:
-                nc.gpsimd.tensor_scalar(
-                    out=unit[:],
-                    in0=centreds[n][:],
-                    scalar1=inverses[i][:, 0:1],
-                    scalar2=0.0,
-                    op0=ALU.mult,
-                    op1=ALU.add,
-                )
-            else:
-                nc.vector.tensor_scalar_mul(
-                    out=unit[:, :VECTOR_SHARE],
-                    in0=centreds[n][:, :VECTOR_SHARE],
-                    scalar1=inverses[i][:, 0:1],
-                )
-                nc.scalar.activation(
-                    out=unit[:, VECTOR_SHARE:],
-                    in_=centreds[n][:, VECTOR_SHARE:],
-                    func=ACT.Copy,
-                    scale=inverses[i][:, 0:1],
-                )
+        def scale_by_vector(n, subtracting):
+            start = GPSIMD_COLUMNS - OVERLAP_COLUMNS if subtracting else 0
+            unit = unit_pool.tile([P, CHUNK], BF16)
+            nc.vector.tensor_scalar_mul(
+                out=unit[:, start:],
+                in0=centreds[n][:, start:],
+                scalar1=inverses[chunks[n][0]][:, 0:1],
+            )
             units[n] = unit
+
+        def scale_by_gpsimd(n):
+            nc.gpsimd.tensor_scalar(
+                out=units[n][:, :GPSIMD_COLUMNS],
+                in0=centreds[n][:, :GPSIMD_COLUMNS],
+                scalar1=inverses[chunks[n][0]][:, 0:1],
+                scalar2=0.0,
+                op0=ALU.mult,
+                op1=ALU.add,
+            )
 
         def transpose(n):
             unit_words = units.pop(n)[:].bitcast(F32)
@@ -224,19 +229,17 @@ def tile_quantumkernelpca_w_kernel(
                 banks.append(bank)
             transposed[n] = banks
 
-        def group(n):
-            grouped = stage_pool.tile([P, CHUNK], BF16, align_bytes=64, name="stage")
-            grouped_words = grouped[:].bitcast(F32).rearrange(
+        def group(n, b, copy):
+            if b == 0:
+                grouped = grouped_pool.tile([P, CHUNK], BF16, align_bytes=64)
+                groupeds[n] = grouped
+            grouped_words = groupeds[n][:].bitcast(F32).rearrange(
                 "p (g r u) -> p g r u", g=CHUNK_PASSES, u=PAIR
             )
-            for b, bank in enumerate(transposed.pop(n)):
-                by_vector = n % VECTOR_COPIES == 0 and b > 0
-                copy = nc.vector.tensor_copy if by_vector else nc.scalar.copy
-                copy(
-                    out=grouped_words[:, b * BANK_PASSES : (b + 1) * BANK_PASSES],
-                    in_=bank[:].rearrange("p g u r -> p g r u"),
-                )
-            groupeds[n] = grouped
+            copy(
+                out=grouped_words[:, b * BANK_PASSES : (b + 1) * BANK_PASSES],
+                in_=transposed[n][b][:].rearrange("p g u r -> p g r u"),
+            )
 
         def quantise(n):
             i, c = chunks[n]
@@ -313,10 +316,28 @@ def tile_quantumkernelpca_w_kernel(
 
             if live(step):
                 fill_mean(chunks[step][1], 1)
+            subtracting = live(step)
+            tile = last_of(step - KERNEL_LAG)
+            if tile is not None and tile > 0 and tile % PACK == 0:
+                quantise_kernel(tile // PACK - 1)
+            if live(step - SCALE_LAG):
+                scale_by_vector(step - SCALE_LAG, subtracting)
             if live(step - QUANTISE_LAG):
                 quantise(step - QUANTISE_LAG)
-            if live(step - GROUP_LAG):
-                group(step - GROUP_LAG)
+            if live(step - SCALE_LAG) and subtracting:
+                scale_by_gpsimd(step - SCALE_LAG)
+
+            normed = last_of(step - NORM_LAG)
+            n = step - GROUP_LAG
+            by_vector = subtracting and n % VECTOR_COPIES == 0
+            if live(n):
+                group(n, 0, nc.scalar.copy)
+            if normed is not None:
+                add_sums(normed)
+            if live(n):
+                group(n, 1, nc.vector.tensor_copy if by_vector else nc.scalar.copy)
+            if normed is not None:
+                root(normed)
             if live(step - TRANSPOSE_LAG):
                 transpose(step - TRANSPOSE_LAG)
             tile = last_of(step - OVERLAP_LAG)
@@ -324,17 +345,15 @@ def tile_quantumkernelpca_w_kernel(
                 square_overlaps(tile // PACK - 1)
             if live(step - QUANTISE_LAG):
                 multiply(step - QUANTISE_LAG)
-            tile = last_of(step - KERNEL_LAG)
-            if tile is not None and tile > 0 and tile % PACK == 0:
-                quantise_kernel(tile // PACK - 1)
-            tile = last_of(step - INVERT_LAG)
-            if tile is not None:
-                invert(tile)
-            if live(step - SCALE_LAG):
-                scale(step - SCALE_LAG, live(step))
-            if live(step):
+
+            if subtracting:
                 centre(step, 0)
+            if normed is not None:
+                add_eps(normed)
+            if subtracting:
                 centre(step, 1)
+            if normed is not None:
+                invert(normed)
             if step + 1 < CHUNKS:
                 widen_mean(step + 1)
                 fill_mean(step + 1, 0)

@@ -37,9 +37,9 @@ HALVES = CHUNK // HALF
 HALF_BLOCKS = HALF // (PAIR * P)
 CHUNK_BLOCKS = CHUNK // (PAIR * P)
 
-GPSIMD_COLUMNS = 1984
+GPSIMD_COLUMNS = 1920
 OVERLAP_COLUMNS = 16
-VECTOR_COPIES = 2
+VECTOR_COPIES, OUT_OF = 3, 8
 
 SQUARE_LAG = 1
 NORM_LAG = 2
@@ -50,6 +50,7 @@ QUANTISE_LAG = 9
 OVERLAP_LAG = 10
 KERNEL_LAG = 13
 LOAD_AHEAD = 6
+BUSY_CHUNKS = 13
 
 FLOPS = 2 * X_ROWS * REF_ROWS * FEATURES + 2 * X_ROWS * REF_ROWS * COMPONENTS
 
@@ -65,7 +66,7 @@ def tile_quantumkernelpca_w_kernel(
     with ExitStack() as ctx:
         const = ctx.enter_context(tc.tile_pool(name="const", bufs=1))
         raw_pool = ctx.enter_context(tc.tile_pool(name="raw", bufs=LOAD_AHEAD + 2))
-        centred_pool = ctx.enter_context(tc.tile_pool(name="centred", bufs=SCALE_LAG + 2))
+        centred_pool = ctx.enter_context(tc.tile_pool(name="centred", bufs=SCALE_LAG + 3))
         squares_pool = ctx.enter_context(tc.tile_pool(name="squares", bufs=2))
         stat_pool = ctx.enter_context(tc.tile_pool(name="stat", bufs=4))
         unit_pool = ctx.enter_context(tc.tile_pool(name="unit", bufs=3))
@@ -85,6 +86,8 @@ def tile_quantumkernelpca_w_kernel(
         identity = const.tile([P, P], F32)
         make_identity(nc, identity[:])
 
+        mean_first = const.tile([P, HALF], BF16)
+        nc.sync.dma_start(out=mean_first[:], in_=mean_[:HALF].partition_broadcast(P))
         mean_words = const.tile([P, WORD_BLOCKS], F32)
         mean_columns = const.tile([P, WORD_BLOCKS, P], F32)
         x_codes = const.tile([P, FEATURE_PASSES * X_ROWS], U32, align_bytes=64)
@@ -123,7 +126,12 @@ def tile_quantumkernelpca_w_kernel(
         def load(n):
             i, c = chunks[n]
             raw = raw_pool.tile([P, CHUNK], BF16)
-            nc.sync.dma_start(out=raw[:], in_=row_tiles[i][:, c * CHUNK : (c + 1) * CHUNK])
+            width = HALF if n == 0 else CHUNK
+            for start in range(0, CHUNK, width):
+                nc.sync.dma_start(
+                    out=raw[:, start : start + width],
+                    in_=row_tiles[i][:, c * CHUNK + start : c * CHUNK + start + width],
+                )
             raws[n] = raw
 
         def spread_mean_words():
@@ -131,11 +139,12 @@ def tile_quantumkernelpca_w_kernel(
             nc.tensor.transpose(bank[:, 0, 0, :], mean_rows[:].bitcast(F32), identity[:])
             nc.vector.tensor_copy(out=mean_words[:], in_=bank[:, 0, 0, :WORD_BLOCKS])
 
-        def widen_mean(c):
-            blocks = slice(c * CHUNK_BLOCKS, (c + 1) * CHUNK_BLOCKS)
-            nc.vector.tensor_copy(
+        def widen_mean(c, h, copy):
+            first = (c * HALVES + h) * HALF_BLOCKS
+            blocks = slice(first, first + HALF_BLOCKS)
+            copy(
                 out=mean_columns[:, blocks, :],
-                in_=mean_words[:, blocks].unsqueeze(2).to_broadcast([P, CHUNK_BLOCKS, P]),
+                in_=mean_words[:, blocks].unsqueeze(2).to_broadcast([P, HALF_BLOCKS, P]),
             )
 
         def fill_mean(c, h):
@@ -153,11 +162,12 @@ def tile_quantumkernelpca_w_kernel(
                 centred = centred_pool.tile([P, CHUNK], F32)
                 centreds[n] = centred
             cols = slice(h * HALF, (h + 1) * HALF)
-            nc.vector.tensor_sub(
-                out=centreds[n][:, cols],
-                in0=raws[n][:, cols],
-                in1=mean_banks[chunks[n][1], h][:].rearrange("p b r -> p (b r)").bitcast(BF16),
-            )
+            if n == 0 and h == 0:
+                means = mean_first[:]
+            else:
+                bank = mean_banks[chunks[n][1], h]
+                means = bank[:].rearrange("p b r -> p (b r)").bitcast(BF16)
+            nc.vector.tensor_sub(out=centreds[n][:, cols], in0=raws[n][:, cols], in1=means)
 
         def square(n):
             i, c = chunks[n]
@@ -220,6 +230,15 @@ def tile_quantumkernelpca_w_kernel(
             banks = []
             for first in range(0, CHUNK_PASSES, BANK_PASSES):
                 bank = transpose_psum.tile([P, BANK_PASSES, PAIR, P], F32)
+                if first == 0 and n >= len(chunks) - BUSY_CHUNKS:
+                    dummy = mean_columns[:, :HALF_BLOCKS, :].rearrange("p b r -> p (b r)").bitcast(BF16)
+                    nc.tensor.matmul(
+                        bank[:].rearrange("p g u r -> p (g u r)"),
+                        lhsT=dummy[:, :P],
+                        rhs=dummy[:, : BANK_PASSES * PAIR * P],
+                        start=True,
+                        stop=True,
+                    )
                 for g in range(BANK_PASSES):
                     for u in range(PAIR):
                         start = ((first + g) * PAIR + u) * P
@@ -306,15 +325,19 @@ def tile_quantumkernelpca_w_kernel(
         for n in range(LOAD_AHEAD):
             load(n)
         spread_mean_words()
-        widen_mean(0)
-        fill_mean(0, 0)
+        widen_mean(0, 1, nc.vector.tensor_copy)
+        fill_mean(0, 1)
+        for c in (1, 2):
+            for h in range(HALVES):
+                widen_mean(c, h, nc.scalar.copy)
+            fill_mean(c, 0)
         for step in range(len(chunks) + KERNEL_LAG + 1):
             if live(step + LOAD_AHEAD):
                 load(step + LOAD_AHEAD)
             if step == 1:
                 load_weight()
 
-            if live(step):
+            if 0 < step < len(chunks):
                 fill_mean(chunks[step][1], 1)
             subtracting = live(step)
             tile = last_of(step - KERNEL_LAG)
@@ -329,7 +352,7 @@ def tile_quantumkernelpca_w_kernel(
 
             normed = last_of(step - NORM_LAG)
             n = step - GROUP_LAG
-            by_vector = subtracting and n % VECTOR_COPIES == 0
+            by_vector = subtracting and n * VECTOR_COPIES % OUT_OF < VECTOR_COPIES
             if live(n):
                 group(n, 0, nc.scalar.copy)
             if normed is not None:
@@ -354,9 +377,13 @@ def tile_quantumkernelpca_w_kernel(
                 centre(step, 1)
             if normed is not None:
                 invert(normed)
-            if step + 1 < CHUNKS:
-                widen_mean(step + 1)
-                fill_mean(step + 1, 0)
+            if step == 1:
+                for h in range(HALVES):
+                    widen_mean(3, h, nc.vector.tensor_copy)
+                fill_mean(3, 0)
+            if step == 2:
+                widen_mean(0, 0, nc.vector.tensor_copy)
+                fill_mean(0, 0)
             if live(step - SQUARE_LAG):
                 square(step - SQUARE_LAG)
 

from contextlib import ExitStack

import concourse.mybir as mybir
from concourse.masks import make_identity

F32 = mybir.dt.float32
BF16 = mybir.dt.bfloat16
I32 = mybir.dt.int32
U32 = mybir.dt.uint32
U8 = mybir.dt.uint8
FP8X4 = mybir.dt.float8_e4m3fn_x4
ACT = mybir.ActivationFunctionType
ALU = mybir.AluOpType

P = 128
PACK = 4
K_PASS = P * PACK

X_ROWS = 128
REF_ROWS = 2048
FEATURES = 8192
COMPONENTS = 128
EPS = 1e-8

FEATURE_PASSES = FEATURES // K_PASS
REF_PASSES = REF_ROWS // K_PASS
ROW_TILES = 1 + REF_ROWS // P

CHUNK = 2048
CHUNKS = FEATURES // CHUNK
CHUNK_PASSES = CHUNK // K_PASS
PAIR = 2
BANK_PASSES = 2
WORD_BLOCKS = FEATURES // PAIR // P
HALF = PAIR * 512
HALVES = CHUNK // HALF
HALF_BLOCKS = HALF // (PAIR * P)
CHUNK_BLOCKS = CHUNK // (PAIR * P)

GPSIMD_COLUMNS = 1920
OVERLAP_COLUMNS = 16
VECTOR_COPIES, OUT_OF = 3, 8

SQUARE_LAG = 1
NORM_LAG = 2
SCALE_LAG = 6
TRANSPOSE_LAG = 7
GROUP_LAG = 8
QUANTISE_LAG = 9
OVERLAP_LAG = 10
KERNEL_LAG = 13
LOAD_AHEAD = 6
BUSY_CHUNKS = 13

FLOPS = 2 * X_ROWS * REF_ROWS * FEATURES + 2 * X_ROWS * REF_ROWS * COMPONENTS


def tile_quantumkernelpca_w_kernel(
    tc, x, x_ref, mean_, components__words, components__scales, out
):
    nc = tc.nc

    ref_tiles = x_ref.rearrange("(g p t) f -> g t p f", p=P, t=PACK)
    row_tiles = [x] + [ref_tiles[g, t] for g in range(REF_PASSES) for t in range(PACK)]

    with ExitStack() as ctx:
        const = ctx.enter_context(tc.tile_pool(name="const", bufs=1))
        raw_pool = ctx.enter_context(tc.tile_pool(name="raw", bufs=LOAD_AHEAD + 2))
        centred_pool = ctx.enter_context(tc.tile_pool(name="centred", bufs=SCALE_LAG + 3))
        squares_pool = ctx.enter_context(tc.tile_pool(name="squares", bufs=2))
        stat_pool = ctx.enter_context(tc.tile_pool(name="stat", bufs=4))
        unit_pool = ctx.enter_context(tc.tile_pool(name="unit", bufs=3))
        grouped_pool = ctx.enter_context(tc.tile_pool(name="grouped", bufs=3))
        codes_pool = ctx.enter_context(tc.tile_pool(name="codes", bufs=2))
        kernel_pool = ctx.enter_context(tc.tile_pool(name="kernel", bufs=2))
        static_psum = ctx.enter_context(tc.psum_pool(name="static_psum", bufs=1))
        transpose_psum = ctx.enter_context(tc.psum_pool(name="transpose_psum", bufs=2))
        mean_psum = ctx.enter_context(tc.psum_pool(name="mean_psum", bufs=1))
        overlap_psum = ctx.enter_context(tc.psum_pool(name="overlap_psum", bufs=1))

        mean_rows = const.tile([P, PAIR * P], BF16)
        nc.vector.memset(mean_rows[:], 0.0)
        nc.sync.dma_start(
            out=mean_rows[:WORD_BLOCKS, :], in_=mean_.rearrange("(b w) -> b w", b=WORD_BLOCKS)
        )
        identity = const.tile([P, P], F32)
        make_identity(nc, identity[:])

        mean_first = const.tile([P, HALF], BF16)
        nc.sync.dma_start(out=mean_first[:], in_=mean_[:HALF].partition_broadcast(P))
        mean_words = const.tile([P, WORD_BLOCKS], F32)
        mean_columns = const.tile([P, WORD_BLOCKS, P], F32)
        x_codes = const.tile([P, FEATURE_PASSES * X_ROWS], U32, align_bytes=64)
        x_scales = const.tile([P, FEATURE_PASSES * X_ROWS], U8, align_bytes=64)
        w_codes = const.tile([P, REF_PASSES * COMPONENTS], U32, align_bytes=64)
        w_scales = const.tile([P, REF_PASSES * COMPONENTS], U8, align_bytes=64)
        kernel_codes = const.tile([P, REF_PASSES * X_ROWS], U32, align_bytes=64)
        kernel_scales = const.tile([P, REF_PASSES * X_ROWS], U8, align_bytes=64)

        nc.vector.memset(w_scales[:].bitcast(I32), 0)

        warm = const.tile([P, 1], F32)
        nc.vector.memset(warm[:], 0.0)
        nc.scalar.activation(out=warm[:], in_=warm[:], func=ACT.Sqrt)

        chunks = [(i, c) for i in range(ROW_TILES) for c in range(CHUNKS)]
        raws, mean_banks, centreds, units, transposed, groupeds = {}, {}, {}, {}, {}, {}
        totals, divisors = {}, {}
        sums, norms, inverses, codes_of, overlaps, kernels = {}, {}, {}, {}, {}, {}

        def load_weight():
            nc.sync.dma_start(
                out=w_codes[:].bitcast(I32).rearrange("p (g n) -> p g n", g=REF_PASSES),
                in_=components__words.rearrange("g p n t -> p g (n t)").bitcast(I32),
            )
            for quadrant in range(4):
                nc.sync.dma_start(
                    out=w_scales[32 * quadrant : 32 * quadrant + 4, :]
                    .bitcast(I32)
                    .rearrange("q (g n) -> q g n", g=REF_PASSES),
                    in_=components__scales[:, 4 * quadrant : 4 * quadrant + 4, :]
                    .rearrange("g q n -> q g n")
                    .bitcast(I32),
                )

        def load(n):
            i, c = chunks[n]
            raw = raw_pool.tile([P, CHUNK], BF16)
            width = HALF if n == 0 else CHUNK
            for start in range(0, CHUNK, width):
                nc.sync.dma_start(
                    out=raw[:, start : start + width],
                    in_=row_tiles[i][:, c * CHUNK + start : c * CHUNK + start + width],
                )
            raws[n] = raw

        def spread_mean_words():
            bank = transpose_psum.tile([P, BANK_PASSES, PAIR, P], F32)
            nc.tensor.transpose(bank[:, 0, 0, :], mean_rows[:].bitcast(F32), identity[:])
            nc.vector.tensor_copy(out=mean_words[:], in_=bank[:, 0, 0, :WORD_BLOCKS])

        def widen_mean(c, h, copy):
            first = (c * HALVES + h) * HALF_BLOCKS
            blocks = slice(first, first + HALF_BLOCKS)
            copy(
                out=mean_columns[:, blocks, :],
                in_=mean_words[:, blocks].unsqueeze(2).to_broadcast([P, HALF_BLOCKS, P]),
            )

        def fill_mean(c, h):
            if h == 0:
                bank = static_psum.tile([P, HALF_BLOCKS, P], F32, name="static_%d" % c)
            else:
                bank = mean_psum.tile([P, HALF_BLOCKS, P], F32, name="mean_bank")
            for b in range(HALF_BLOCKS):
                block = (c * HALVES + h) * HALF_BLOCKS + b
                nc.tensor.transpose(bank[:, b, :], mean_columns[:, block, :], identity[:])
            mean_banks[c, h] = bank

        def centre(n, h):
            if h == 0:
                centred = centred_pool.tile([P, CHUNK], F32)
                centreds[n] = centred
            cols = slice(h * HALF, (h + 1) * HALF)
            if n == 0 and h == 0:
                means = mean_first[:]
            else:
                bank = mean_banks[chunks[n][1], h]
                means = bank[:].rearrange("p b r -> p (b r)").bitcast(BF16)
            nc.vector.tensor_sub(out=centreds[n][:, cols], in0=raws[n][:, cols], in1=means)

        def square(n):
            i, c = chunks[n]
            if c == 0:
                tile_sums = stat_pool.tile([P, CHUNKS], F32)
                sums[i] = tile_sums
            squares = squares_pool.tile([P, CHUNK], BF16)
            nc.scalar.activation(
                out=squares[:],
                in_=centreds[n][:],
                func=ACT.Square,
                accum_out=sums[i][:, c : c + 1],
            )

        def add_sums(i):
            sums_again = stat_pool.tile([P, CHUNKS], F32)
            total = stat_pool.tile([P, 1], F32)
            nc.scalar.activation(
                out=sums_again[:], in_=sums[i][:], func=ACT.Copy, accum_out=total[:]
            )
            totals[i] = total

        def root(i):
            norm = stat_pool.tile([P, 1], F32)
            nc.scalar.activation(out=norm[:], in_=totals[i][:], func=ACT.Sqrt)
            norms[i] = norm

        def add_eps(i):
            divisor = stat_pool.tile([P, 1], F32)
            nc.vector.tensor_scalar_add(out=divisor[:], in0=norms[i][:], scalar1=EPS)
            divisors[i] = divisor

        def invert(i):
            inverse = stat_pool.tile([P, 1], F32)
            nc.vector.reciprocal(out=inverse[:], in_=divisors[i][:])
            inverses[i] = inverse

        def scale_by_vector(n, subtracting):
            start = GPSIMD_COLUMNS - OVERLAP_COLUMNS if subtracting else 0
            unit = unit_pool.tile([P, CHUNK], BF16)
            nc.vector.tensor_scalar_mul(
                out=unit[:, start:],
                in0=centreds[n][:, start:],
                scalar1=inverses[chunks[n][0]][:, 0:1],
            )
            units[n] = unit

        def scale_by_gpsimd(n):
            nc.gpsimd.tensor_scalar(
                out=units[n][:, :GPSIMD_COLUMNS],
                in0=centreds[n][:, :GPSIMD_COLUMNS],
                scalar1=inverses[chunks[n][0]][:, 0:1],
                scalar2=0.0,
                op0=ALU.mult,
                op1=ALU.add,
            )

        def transpose(n):
            unit_words = units.pop(n)[:].bitcast(F32)
            banks = []
            for first in range(0, CHUNK_PASSES, BANK_PASSES):
                bank = transpose_psum.tile([P, BANK_PASSES, PAIR, P], F32)
                if first == 0 and n >= len(chunks) - BUSY_CHUNKS:
                    dummy = mean_columns[:, :HALF_BLOCKS, :].rearrange("p b r -> p (b r)").bitcast(BF16)
                    nc.tensor.matmul(
                        bank[:].rearrange("p g u r -> p (g u r)"),
                        lhsT=dummy[:, :P],
                        rhs=dummy[:, : BANK_PASSES * PAIR * P],
                        start=True,
                        stop=True,
                    )
                for g in range(BANK_PASSES):
                    for u in range(PAIR):
                        start = ((first + g) * PAIR + u) * P
                        nc.tensor.transpose(
                            bank[:, g, u, :], unit_words[:, start : start + P], identity[:]
                        )
                banks.append(bank)
            transposed[n] = banks

        def group(n, b, copy):
            if b == 0:
                grouped = grouped_pool.tile([P, CHUNK], BF16, align_bytes=64)
                groupeds[n] = grouped
            grouped_words = groupeds[n][:].bitcast(F32).rearrange(
                "p (g r u) -> p g r u", g=CHUNK_PASSES, u=PAIR
            )
            copy(
                out=grouped_words[:, b * BANK_PASSES : (b + 1) * BANK_PASSES],
                in_=transposed[n][b][:].rearrange("p g u r -> p g r u"),
            )

        def quantise(n):
            i, c = chunks[n]
            if c == 0:
                if i == 0:
                    codes_of[i] = (x_codes, x_scales)
                else:
                    codes = codes_pool.tile([P, FEATURE_PASSES * P], U32, align_bytes=64)
                    scales = codes_pool.tile([P, FEATURE_PASSES * P], U8, align_bytes=64)
                    codes_of[i] = (codes, scales)
            tile_codes, tile_scales = codes_of[i]
            words = slice(c * CHUNK_PASSES * P, (c + 1) * CHUNK_PASSES * P)
            nc.vector.quantize_mx(
                out=tile_codes[:, words].bitcast(FP8X4),
                scales=tile_scales[:, words],
                in_=groupeds.pop(n)[:],
            )

        def multiply(n):
            i, c = chunks[n]
            if i == 0:
                return
            group_of_i, t = divmod(i - 1, PACK)
            if c == 0 and t == 0:
                overlap = overlap_psum.tile([P, PACK, X_ROWS], F32)
                overlaps[group_of_i] = overlap
            tile_codes, tile_scales = codes_of[i]
            for g in range(c * CHUNK_PASSES, (c + 1) * CHUNK_PASSES):
                words = slice(g * P, (g + 1) * P)
                nc.tensor.matmul_mx(
                    out=overlaps[group_of_i][:, t, :],
                    lhsT=tile_codes[:, words].bitcast(FP8X4),
                    lhsT_scale=tile_scales[:, words],
                    rhs=x_codes[:, words].bitcast(FP8X4),
                    rhs_scale=x_scales[:, words],
                    start=(g == 0),
                    stop=(g == FEATURE_PASSES - 1),
                )

        def square_overlaps(g):
            kernel_grouped = kernel_pool.tile([P, X_ROWS, PACK], BF16, align_bytes=64)
            nc.scalar.activation(
                out=kernel_grouped[:],
                in_=overlaps.pop(g)[:].rearrange("p t n -> p n t"),
                func=ACT.Square,
            )
            kernels[g] = kernel_grouped

        def quantise_kernel(g):
            words = slice(g * X_ROWS, (g + 1) * X_ROWS)
            nc.vector.quantize_mx(
                out=kernel_codes[:, words].bitcast(FP8X4),
                scales=kernel_scales[:, words],
                in_=kernels.pop(g)[:].rearrange("p n t -> p (n t)"),
            )

        def live(n):
            return 0 <= n < len(chunks)

        def last_of(n):
            return n // CHUNKS if live(n) and n % CHUNKS == CHUNKS - 1 else None

        ctx.enter_context(tc.manual_schedule())
        for n in range(LOAD_AHEAD):
            load(n)
        spread_mean_words()
        widen_mean(0, 1, nc.vector.tensor_copy)
        fill_mean(0, 1)
        for c in (1, 2):
            for h in range(HALVES):
                widen_mean(c, h, nc.scalar.copy)
            fill_mean(c, 0)
        for step in range(len(chunks) + KERNEL_LAG + 1):
            if live(step + LOAD_AHEAD):
                load(step + LOAD_AHEAD)
            if step == 1:
                load_weight()

            if 0 < step < len(chunks):
                fill_mean(chunks[step][1], 1)
            subtracting = live(step)
            tile = last_of(step - KERNEL_LAG)
            if tile is not None and tile > 0 and tile % PACK == 0:
                quantise_kernel(tile // PACK - 1)
            if live(step - SCALE_LAG):
                scale_by_vector(step - SCALE_LAG, subtracting)
            if live(step - QUANTISE_LAG):
                quantise(step - QUANTISE_LAG)
            if live(step - SCALE_LAG) and subtracting:
                scale_by_gpsimd(step - SCALE_LAG)

            normed = last_of(step - NORM_LAG)
            n = step - GROUP_LAG
            by_vector = subtracting and n * VECTOR_COPIES % OUT_OF < VECTOR_COPIES
            if live(n):
                group(n, 0, nc.scalar.copy)
            if normed is not None:
                add_sums(normed)
            if live(n):
                group(n, 1, nc.vector.tensor_copy if by_vector else nc.scalar.copy)
            if normed is not None:
                root(normed)
            if live(step - TRANSPOSE_LAG):
                transpose(step - TRANSPOSE_LAG)
            tile = last_of(step - OVERLAP_LAG)
            if tile is not None and tile > 0 and tile % PACK == 0:
                square_overlaps(tile // PACK - 1)
            if live(step - QUANTISE_LAG):
                multiply(step - QUANTISE_LAG)

            if subtracting:
                centre(step, 0)
            if normed is not None:
                add_eps(normed)
            if subtracting:
                centre(step, 1)
            if normed is not None:
                invert(normed)
            if step == 1:
                for h in range(HALVES):
                    widen_mean(3, h, nc.vector.tensor_copy)
                fill_mean(3, 0)
            if step == 2:
                widen_mean(0, 0, nc.vector.tensor_copy)
                fill_mean(0, 0)
            if live(step - SQUARE_LAG):
                square(step - SQUARE_LAG)

        bank = transpose_psum.tile([P, BANK_PASSES, PAIR, P], F32)
        overlap = bank[:, 0, 0, :]
        for g in range(REF_PASSES):
            words = slice(g * X_ROWS, (g + 1) * X_ROWS)
            nc.tensor.matmul_mx(
                out=overlap,
                lhsT=kernel_codes[:, words].bitcast(FP8X4),
                lhsT_scale=kernel_scales[:, words],
                rhs=w_codes[:, words].bitcast(FP8X4),
                rhs_scale=w_scales[:, words],
                start=(g == 0),
                stop=(g == REF_PASSES - 1),
            )
        result = const.tile([X_ROWS, COMPONENTS], F32)
        nc.vector.tensor_copy(out=result[:], in_=overlap)
        nc.sync.dma_start(out=out, in_=result[:])
